import numpy as np
import ml_dtypes

BF16 = ml_dtypes.bfloat16


def bf(x):
    return np.asarray(x, np.float32).astype(BF16)


def f32(x):
    return np.asarray(x, np.float32)


def f64(x):
    return np.asarray(x).astype(np.float64)


def striped(idx):
    return np.tile(idx.reshape(-1, 16).T, (8, 1))


C, S, N, H, HD, WIN, B, NB, SPAN = 512, 2048, 2048, 4, 128, 256, 128, 16, 384


def setup_inputs():
    x = f32(np.random.standard_normal((C, S)))
    wq = bf(1.2 * np.random.standard_normal((C, C)) / np.sqrt(C))
    bq = f32(0.1 * np.random.standard_normal((C, 1)))
    wk = bf(1.2 * np.random.standard_normal((C, C)) / np.sqrt(C))
    wv = bf(2.0 * np.random.standard_normal((C, C)) / np.sqrt(C))
    bv = f32(0.1 * np.random.standard_normal((C, 1)))
    wo = bf(2.0 * np.random.standard_normal((C, C)) / np.sqrt(C))
    bo = f32(0.1 * np.random.standard_normal((C, 1)))
    return {"x": x, "wq": wq, "bq": bq, "wk": wk, "wv": wv, "bv": bv, "wo": wo, "bo": bo, "offs": striped(np.random.permutation(S)[:N])}


def reference(x, wq, bq, wk, wv, bv, wo, bo, offs):
    idx = offs[:16].T.reshape(-1)
    xo = f64(x)[:, idx]
    q = f64(wq).T @ xo + f64(bq)
    k = f64(wk).T @ xo
    v = f64(wv).T @ xo + f64(bv)
    i = np.arange(B)[:, None]
    r = np.arange(SPAN)[None, :]
    valid = (r >= i) & (r <= i + WIN)
    a = np.zeros((C, N))
    for n in range(NB):
        cols = (n * B - B + np.arange(SPAN)) % N
        for h in range(H):
            rows = slice(h * HD, (h + 1) * HD)
            s = q[rows, n * B:(n + 1) * B].T @ k[rows][:, cols] / np.sqrt(HD)
            s = np.where(valid, s, -1e30)
            e = np.exp(s - s.max(axis=1, keepdims=True))
            p = e / e.sum(axis=1, keepdims=True)
            a[rows, n * B:(n + 1) * B] = v[rows][:, cols] @ p.T
    return f64(wo).T @ a + f64(bo)

@@ -1,0 +1,225 @@
+import math
+
+import concourse.mybir as mybir
+from concourse.masks import make_identity
+
+F32, BF16, U16 = mybir.dt.float32, mybir.dt.bfloat16, mybir.dt.uint16
+ACT = mybir.ActivationFunctionType
+ALU = mybir.AluOpType
+
+P = 128
+C = 512
+N = 2048
+H = C // P
+NB = N // P
+PIECE = 512
+NP = N // PIECE
+BPP = PIECE // P
+SPAN = 3 * P
+VW = 136
+
+FLOPS = 4 * 2 * C * C * N + 2 * 2 * H * N * 257 * P
+
+
+def ring_runs(first, count):
+    first = first % NB
+    if first + count <= NB:
+        return [(first, count)]
+    return [(first, NB - first), (0, first + count - NB)]
+
+
+def tile_slidingwindowattention_b_kernel(tc, x, wq, bq, wk, wv, bv, wo, bo, offs, out):
+    nc = tc.nc
+    with (
+        tc.tile_pool(name="held", bufs=1) as held,
+        tc.tile_pool(name="picked", bufs=4) as picked,
+        tc.tile_pool(name="work", bufs=2) as work,
+        tc.tile_pool(name="staged", bufs=3) as staged,
+        tc.psum_pool(name="acc_pool", bufs=2) as acc_pool,
+        tc.psum_pool(name="score_pool", bufs=3) as score_pool,
+        tc.psum_pool(name="mix_pool", bufs=2) as mix_pool,
+        tc.psum_pool(name="flip_pool", bufs=1) as flip_pool,
+    ):
+        offsets = held.tile([P, N // 16], U16, name="offsets")
+        nc.sync.dma_start(offsets[:], offs)
+        x_sb = [held.tile([P, N], F32, name=f"x{c}") for c in range(H)]
+        for c in range(H):
+            nc.sync.dma_start(x_sb[c][:], x[c * P : (c + 1) * P, :])
+        w_sb = {}
+        for name, w in (("q", wq), ("k", wk), ("v", wv), ("o", wo)):
+            w_sb[name] = held.tile([P, H, C], BF16, name=f"w{name}")
+            nc.sync.dma_start(w_sb[name][:], w.rearrange("(c p) m -> p c m", p=P))
+        b_sb = {}
+        with nc.allow_non_contiguous_dma(reason="a bias lies one value to a partition"):
+            for name, b in (("q", bq), ("v", bv), ("o", bo)):
+                b_sb[name] = held.tile([P, H], F32, name=f"b{name}")
+                nc.scalar.dma_start(b_sb[name][:], b.rearrange("(a p) o -> p (a o)", p=P))
+
+        ident_bf = held.tile([P, P], BF16, name="ident_bf")
+        make_identity(nc, ident_bf[:])
+        ident_f32 = held.tile([P, P], F32, name="ident_f32")
+        make_identity(nc, ident_f32[:])
+
+        acc = acc_pool.tile([P, PIECE], F32)
+        for h in range(H):
+            nc.tensor.matmul(
+                acc[:, h * P : (h + 1) * P],
+                lhsT=b_sb["v"][:, h : h + 1].to_broadcast([P, P]),
+                rhs=ident_f32[:],
+                start=True,
+                stop=True,
+            )
+        bv_all = held.tile([P, C], F32, name="bv_all")
+        nc.vector.tensor_copy(bv_all[:], acc[:])
+
+        xo = held.tile([P, H, N], BF16, name="xo")
+        q_sb = held.tile([P, H, N], BF16, name="q_sb")
+        k_sb = held.tile([P, H, N], BF16, name="k_sb")
+        v_sb = held.tile([P, NB, H, VW], BF16, name="v_sb")
+        a_sb = held.tile([P, H, N], BF16, name="a_sb")
+        e_sb = [held.tile([P, H, SPAN], BF16, name=f"e{tb}") for tb in range(NB)]
+        nc.vector.memset(v_sb[:, :, :, P : P + 1], 1.0)
+
+        def gather(tp):
+            for c in range(H):
+                xo32 = picked.tile([P, PIECE], F32)
+                nc.scalar.activation(
+                    xo32[:],
+                    x_sb[c][:].indirect(offsets[:, tp * (PIECE // 16) : (tp + 1) * (PIECE // 16)]),
+                    ACT.Copy,
+                )
+                nc.vector.tensor_copy(xo[:, c, tp * PIECE : (tp + 1) * PIECE], xo32[:])
+
+        def project(tp):
+            cols = slice(tp * PIECE, (tp + 1) * PIECE)
+            for name in ("q", "k"):
+                for m in range(H):
+                    acc = acc_pool.tile([P, PIECE], F32)
+                    for c in range(H):
+                        nc.tensor.matmul(
+                            acc[:],
+                            lhsT=w_sb[name][:, c, m * P : (m + 1) * P],
+                            rhs=xo[:, c, cols],
+                            start=(c == 0),
+                            stop=(c == H - 1),
+                        )
+                    if name == "q":
+                        nc.scalar.activation(q_sb[:, m, cols], acc[:], ACT.Identity, bias=b_sb["q"][:, m : m + 1])
+                    else:
+                        nc.vector.tensor_copy(k_sb[:, m, cols], acc[:])
+            for tb in range(tp * BPP, (tp + 1) * BPP):
+                acc = acc_pool.tile([P, PIECE], F32)
+                for c in range(H):
+                    nc.tensor.matmul(
+                        acc[:],
+                        lhsT=xo[:, c, tb * P : (tb + 1) * P],
+                        rhs=w_sb["v"][:, c, :],
+                        start=(c == 0),
+                        stop=(c == H - 1),
+                    )
+                nc.vector.tensor_tensor(
+                    v_sb[:, tb, :, 0:P],
+                    acc[:].rearrange("p (h d) -> p h d", h=H),
+                    bv_all[:].rearrange("p (h d) -> p h d", h=H),
+                    ALU.add,
+                )
+
+        def scores(tb):
+            for h in range(H):
+                s_ps = score_pool.tile([P, SPAN], F32)
+                at = 0
+                for first, count in ring_runs(tb - 1, 3):
+                    nc.tensor.matmul(
+                        s_ps[:, at : at + count * P],
+                        lhsT=k_sb[:, h, tb * P : (tb + 1) * P],
+                        rhs=q_sb[:, h, first * P : (first + count) * P],
+                        start=True,
+                        stop=True,
+                    )
+                    at += count * P
+                nc.scalar.activation(e_sb[tb][:, h, :], s_ps[:], ACT.Exp, scale=1.0 / math.sqrt(P))
+            nc.gpsimd.affine_select(
+                out=e_sb[tb][:, :, 0:P],
+                in_=e_sb[tb][:, :, 0:P],
+                pattern=[[0, H], [1, P]],
+                compare_op=ALU.is_ge,
+                fill=0.0,
+                base=0,
+                channel_multiplier=-1,
+            )
+            nc.gpsimd.affine_select(
+                out=e_sb[tb][:, :, 2 * P : 3 * P],
+                in_=e_sb[tb][:, :, 2 * P : 3 * P],
+                pattern=[[0, H], [-1, P]],
+                compare_op=ALU.is_ge,
+                fill=0.0,
+                base=0,
+                channel_multiplier=1,
+            )
+
+        def attend(jb):
+            a_tok = work.tile([P, H, P], BF16)
+            for pair in range(H // 2):
+                mix = mix_pool.tile([P, 2, PIECE // 2], F32)
+                for i in range(2):
+                    h = 2 * pair + i
+                    for r in range(3):
+                        tb = (jb - 1 + r) % NB
+                        nc.tensor.matmul(
+                            mix[:, i, 0 : P + 1],
+                            lhsT=e_sb[tb][:, h, (2 - r) * P : (3 - r) * P],
+                            rhs=v_sb[:, tb, h, 0 : P + 1],
+                            start=(r == 0),
+                            stop=(r == 2),
+                        )
+                inv = work.tile([P, 2, 1], F32)
+                nc.vector.reciprocal(inv[:], mix[:, :, P : P + 1])
+                nc.vector.tensor_tensor(
+                    a_tok[:, 2 * pair : 2 * pair + 2, :], mix[:, :, 0:P], inv[:].to_broadcast([P, 2, P]), ALU.mult
+                )
+            flip = flip_pool.tile([P, H, P], BF16)
+            for h in range(H):
+                nc.tensor.transpose(flip[:, h, :], a_tok[:, h, :], ident_bf[:])
+            nc.vector.tensor_copy(a_sb[:, :, jb * P : (jb + 1) * P], flip[:])
+
+        def project_out(tp):
+            cols = slice(tp * PIECE, (tp + 1) * PIECE)
+            for m in range(H):
+                acc = acc_pool.tile([P, PIECE], F32)
+                for h in range(H):
+                    nc.tensor.matmul(
+                        acc[:],
+                        lhsT=w_sb["o"][:, h, m * P : (m + 1) * P],
+                        rhs=a_sb[:, h, cols],
+                        start=(h == 0),
+                        stop=(h == H - 1),
+                    )
+                o_sb = staged.tile([P, PIECE], F32)
+                nc.vector.tensor_scalar_add(o_sb[:], acc[:], b_sb["o"][:, m : m + 1])
+                nc.sync.dma_start(out[m * P : (m + 1) * P, cols], o_sb[:])
+
+        gather(0)
+        gather(1)
+        project(0)
+        gather(2)
+        project(1)
+        gather(3)
+        for tb in (1, 2):
+            scores(tb)
+        for tb in (3, 4, 5, 6):
+            scores(tb)
+            attend(tb - 1)
+        project(2)
+        for tb in (7, 8, 9, 10):
+            scores(tb)
+            attend(tb - 1)
+        project_out(1)
+        project(3)
+        for tb in (11, 12, 13, 14, 15, 0):
+            scores(tb)
+            attend((tb - 1) % NB)
+        project_out(2)
+        attend(0)
+        attend(1)
+        project_out(3)
+        project_out(0)

@@ -13,7 +13,6 @@ N = 2048
 H = C // P
 NB = N // P
 PIECE = 512
-NP = N // PIECE
 BPP = PIECE // P
 SPAN = 3 * P
 VW = 136
@@ -33,34 +32,37 @@ def tile_slidingwindowattention_b_kernel(tc, x, wq, bq, wk, wv, bv, wo, bo, offs
     with (
         tc.tile_pool(name="held", bufs=1) as held,
         tc.tile_pool(name="picked", bufs=4) as picked,
-        tc.tile_pool(name="work", bufs=2) as work,
-        tc.tile_pool(name="staged", bufs=3) as staged,
-        tc.psum_pool(name="acc_pool", bufs=2) as acc_pool,
-        tc.psum_pool(name="score_pool", bufs=3) as score_pool,
-        tc.psum_pool(name="mix_pool", bufs=2) as mix_pool,
-        tc.psum_pool(name="flip_pool", bufs=1) as flip_pool,
+        tc.tile_pool(name="work", bufs=3) as work,
+        tc.tile_pool(name="staged", bufs=4) as staged,
+        tc.psum_pool(name="psum", bufs=8) as psum,
     ):
         offsets = held.tile([P, N // 16], U16, name="offsets")
         nc.sync.dma_start(offsets[:], offs)
         x_sb = [held.tile([P, N], F32, name=f"x{c}") for c in range(H)]
-        for c in range(H):
+        w_sb = {name: held.tile([P, H, C], BF16, name=f"w{name}") for name in ("q", "k", "v", "o")}
+        nc.sync.dma_start(x_sb[0][:], x[0:P, :])
+        nc.sync.dma_start(w_sb["q"][:], wq.rearrange("(c p) m -> p c m", p=P))
+        nc.sync.dma_start(w_sb["k"][:], wk.rearrange("(c p) m -> p c m", p=P))
+        for c in range(1, H):
             nc.sync.dma_start(x_sb[c][:], x[c * P : (c + 1) * P, :])
-        w_sb = {}
-        for name, w in (("q", wq), ("k", wk), ("v", wv), ("o", wo)):
-            w_sb[name] = held.tile([P, H, C], BF16, name=f"w{name}")
-            nc.sync.dma_start(w_sb[name][:], w.rearrange("(c p) m -> p c m", p=P))
+        nc.sync.dma_start(w_sb["v"][:], wv.rearrange("(c p) m -> p c m", p=P))
+        nc.sync.dma_start(w_sb["o"][:], wo.rearrange("(c p) m -> p c m", p=P))
         b_sb = {}
         with nc.allow_non_contiguous_dma(reason="a bias lies one value to a partition"):
-            for name, b in (("q", bq), ("v", bv), ("o", bo)):
+            for name, bias in (("v", bv), ("q", bq), ("o", bo)):
                 b_sb[name] = held.tile([P, H], F32, name=f"b{name}")
-                nc.scalar.dma_start(b_sb[name][:], b.rearrange("(a p) o -> p (a o)", p=P))
+                nc.scalar.dma_start(b_sb[name][:], bias.rearrange("(a p) o -> p (a o)", p=P))
 
-        ident_bf = held.tile([P, P], BF16, name="ident_bf")
-        make_identity(nc, ident_bf[:])
+        warm = held.tile([P, 1], F32, name="warm")
+        nc.vector.memset(warm[:], 0.0)
+        nc.scalar.activation(warm[:], warm[:], ACT.Exp)
+
         ident_f32 = held.tile([P, P], F32, name="ident_f32")
         make_identity(nc, ident_f32[:])
+        ident_bf = held.tile([P, P], BF16, name="ident_bf")
+        make_identity(nc, ident_bf[:])
 
-        acc = acc_pool.tile([P, PIECE], F32)
+        acc = psum.tile([P, PIECE], F32, name="bank")
         for h in range(H):
             nc.tensor.matmul(
                 acc[:, h * P : (h + 1) * P],
@@ -80,64 +82,63 @@ def tile_slidingwindowattention_b_kernel(tc, x, wq, bq, wk, wv, bv, wo, bo, offs
         e_sb = [held.tile([P, H, SPAN], BF16, name=f"e{tb}") for tb in range(NB)]
         nc.vector.memset(v_sb[:, :, :, P : P + 1], 1.0)
 
-        def gather(tp):
-            for c in range(H):
-                xo32 = picked.tile([P, PIECE], F32)
-                nc.scalar.activation(
-                    xo32[:],
-                    x_sb[c][:].indirect(offsets[:, tp * (PIECE // 16) : (tp + 1) * (PIECE // 16)]),
-                    ACT.Copy,
-                )
-                nc.vector.tensor_copy(xo[:, c, tp * PIECE : (tp + 1) * PIECE], xo32[:])
+        def gather(tp, c):
+            xo32 = picked.tile([P, PIECE], F32)
+            nc.scalar.activation(
+                xo32[:],
+                x_sb[c][:].indirect(offsets[:, tp * (PIECE // 16) : (tp + 1) * (PIECE // 16)]),
+                ACT.Copy,
+            )
+            nc.vector.tensor_copy(xo[:, c, tp * PIECE : (tp + 1) * PIECE], xo32[:])
 
-        def project(tp):
+        def project_qk(name, tp, m, c, acc):
+            nc.tensor.matmul(
+                acc[:],
+                lhsT=w_sb[name][:, c, m * P : (m + 1) * P],
+                rhs=xo[:, c, tp * PIECE : (tp + 1) * PIECE],
+                start=(c == 0),
+                stop=(c == H - 1),
+            )
+
+        def keep_qk(name, tp, m, acc):
             cols = slice(tp * PIECE, (tp + 1) * PIECE)
-            for name in ("q", "k"):
-                for m in range(H):
-                    acc = acc_pool.tile([P, PIECE], F32)
-                    for c in range(H):
-                        nc.tensor.matmul(
-                            acc[:],
-                            lhsT=w_sb[name][:, c, m * P : (m + 1) * P],
-                            rhs=xo[:, c, cols],
-                            start=(c == 0),
-                            stop=(c == H - 1),
-                        )
-                    if name == "q":
-                        nc.scalar.activation(q_sb[:, m, cols], acc[:], ACT.Identity, bias=b_sb["q"][:, m : m + 1])
-                    else:
-                        nc.vector.tensor_copy(k_sb[:, m, cols], acc[:])
-            for tb in range(tp * BPP, (tp + 1) * BPP):
-                acc = acc_pool.tile([P, PIECE], F32)
-                for c in range(H):
-                    nc.tensor.matmul(
-                        acc[:],
-                        lhsT=xo[:, c, tb * P : (tb + 1) * P],
-                        rhs=w_sb["v"][:, c, :],
-                        start=(c == 0),
-                        stop=(c == H - 1),
-                    )
-                nc.vector.tensor_tensor(
-                    v_sb[:, tb, :, 0:P],
-                    acc[:].rearrange("p (h d) -> p h d", h=H),
-                    bv_all[:].rearrange("p (h d) -> p h d", h=H),
-                    ALU.add,
-                )
+            if name == "q":
+                nc.vector.tensor_scalar_add(q_sb[:, m, cols], acc[:], b_sb["q"][:, m : m + 1])
+            else:
+                nc.vector.tensor_copy(k_sb[:, m, cols], acc[:])
 
-        def scores(tb):
-            for h in range(H):
-                s_ps = score_pool.tile([P, SPAN], F32)
-                at = 0
-                for first, count in ring_runs(tb - 1, 3):
-                    nc.tensor.matmul(
-                        s_ps[:, at : at + count * P],
-                        lhsT=k_sb[:, h, tb * P : (tb + 1) * P],
-                        rhs=q_sb[:, h, first * P : (first + count) * P],
-                        start=True,
-                        stop=True,
-                    )
-                    at += count * P
-                nc.scalar.activation(e_sb[tb][:, h, :], s_ps[:], ACT.Exp, scale=1.0 / math.sqrt(P))
+        def project_v(tb):
+            acc = psum.tile([P, PIECE], F32, name="bank")
+            for c in range(H):
+                nc.tensor.matmul(
+                    acc[:],
+                    lhsT=xo[:, c, tb * P : (tb + 1) * P],
+                    rhs=w_sb["v"][:, c, :],
+                    start=(c == 0),
+                    stop=(c == H - 1),
+                )
+            nc.vector.tensor_tensor(
+                v_sb[:, tb, :, 0:P],
+                acc[:].rearrange("p (h d) -> p h d", h=H),
+                bv_all[:].rearrange("p (h d) -> p h d", h=H),
+                ALU.add,
+            )
+
+        def score(tb, h):
+            s_ps = psum.tile([P, SPAN], F32, name="bank")
+            at = 0
+            for first, count in ring_runs(tb - 1, 3):
+                nc.tensor.matmul(
+                    s_ps[:, at : at + count * P],
+                    lhsT=k_sb[:, h, tb * P : (tb + 1) * P],
+                    rhs=q_sb[:, h, first * P : (first + count) * P],
+                    start=True,
+                    stop=True,
+                )
+                at += count * P
+            nc.scalar.activation(e_sb[tb][:, h, :], s_ps[:], ACT.Exp, scale=1.0 / math.sqrt(P))
+
+        def mask(tb):
             nc.gpsimd.affine_select(
                 out=e_sb[tb][:, :, 0:P],
                 in_=e_sb[tb][:, :, 0:P],
@@ -157,69 +158,80 @@ def tile_slidingwindowattention_b_kernel(tc, x, wq, bq, wk, wv, bv, wo, bo, offs
                 channel_multiplier=1,
             )
 
-        def attend(jb):
-            a_tok = work.tile([P, H, P], BF16)
-            for pair in range(H // 2):
-                mix = mix_pool.tile([P, 2, PIECE // 2], F32)
-                for i in range(2):
-                    h = 2 * pair + i
-                    for r in range(3):
-                        tb = (jb - 1 + r) % NB
-                        nc.tensor.matmul(
-                            mix[:, i, 0 : P + 1],
-                            lhsT=e_sb[tb][:, h, (2 - r) * P : (3 - r) * P],
-                            rhs=v_sb[:, tb, h, 0 : P + 1],
-                            start=(r == 0),
-                            stop=(r == 2),
-                        )
-                inv = work.tile([P, 2, 1], F32)
-                nc.vector.reciprocal(inv[:], mix[:, :, P : P + 1])
-                nc.vector.tensor_tensor(
-                    a_tok[:, 2 * pair : 2 * pair + 2, :], mix[:, :, 0:P], inv[:].to_broadcast([P, 2, P]), ALU.mult
+        def attend(jb, h, mix):
+            for r in range(3):
+                tb = (jb - 1 + r) % NB
+                nc.tensor.matmul(
+                    mix[:, h % 2, 0 : P + 1],
+                    lhsT=e_sb[tb][:, h, (2 - r) * P : (3 - r) * P],
+                    rhs=v_sb[:, tb, h, 0 : P + 1],
+                    start=(r == 0),
+                    stop=(r == 2),
                 )
-            flip = flip_pool.tile([P, H, P], BF16)
+
+        def normalise(mix, a_pair):
+            inv = work.tile([P, 2, 1], F32)
+            nc.vector.reciprocal(inv[:], mix[:, :, P : P + 1])
+            nc.vector.tensor_tensor(a_pair, mix[:, :, 0:P], inv[:].to_broadcast([P, 2, P]), ALU.mult)
+
+        def project_out(g, m):
+            acc = psum.tile([P, PIECE], F32, name="bank")
             for h in range(H):
-                nc.tensor.transpose(flip[:, h, :], a_tok[:, h, :], ident_bf[:])
-            nc.vector.tensor_copy(a_sb[:, :, jb * P : (jb + 1) * P], flip[:])
+                nc.tensor.matmul(
+                    acc[:],
+                    lhsT=w_sb["o"][:, h, m * P : (m + 1) * P],
+                    rhs=a_sb[:, h, g * PIECE : (g + 1) * PIECE],
+                    start=(h == 0),
+                    stop=(h == H - 1),
+                )
+            o_sb = staged.tile([P, PIECE], F32)
+            nc.scalar.activation(o_sb[:], acc[:], ACT.Identity, bias=b_sb["o"][:, m : m + 1])
+            at = 0
+            for first, count in ring_runs(g * BPP + 2, BPP):
+                nc.sync.dma_start(
+                    out[m * P : (m + 1) * P, first * P : (first + count) * P], o_sb[:, at : at + count * P]
+                )
+                at += count * P
 
-        def project_out(tp):
-            cols = slice(tp * PIECE, (tp + 1) * PIECE)
-            for m in range(H):
-                acc = acc_pool.tile([P, PIECE], F32)
-                for h in range(H):
-                    nc.tensor.matmul(
-                        acc[:],
-                        lhsT=w_sb["o"][:, h, m * P : (m + 1) * P],
-                        rhs=a_sb[:, h, cols],
-                        start=(h == 0),
-                        stop=(h == H - 1),
-                    )
-                o_sb = staged.tile([P, PIECE], F32)
-                nc.vector.tensor_scalar_add(o_sb[:], acc[:], b_sb["o"][:, m : m + 1])
-                nc.sync.dma_start(out[m * P : (m + 1) * P, cols], o_sb[:])
+        first_banks = [(name, m, psum.tile([P, PIECE], F32, name="bank")) for name in ("q", "k") for m in range(H)]
+        for c in range(H):
+            gather(0, c)
+            for name, m, acc in first_banks:
+                project_qk(name, 0, m, c, acc)
+        for name, m, acc in first_banks:
+            keep_qk(name, 0, m, acc)
 
-        gather(0)
-        gather(1)
-        project(0)
-        gather(2)
-        project(1)
-        gather(3)
-        for tb in (1, 2):
-            scores(tb)
-        for tb in (3, 4, 5, 6):
-            scores(tb)
-            attend(tb - 1)
-        project(2)
-        for tb in (7, 8, 9, 10):
-            scores(tb)
-            attend(tb - 1)
-        project_out(1)
-        project(3)
-        for tb in (11, 12, 13, 14, 15, 0):
-            scores(tb)
-            attend((tb - 1) % NB)
-        project_out(2)
-        attend(0)
-        attend(1)
-        project_out(3)
-        project_out(0)
+        a_tok = {}
+        for step in range(NB + 16):
+            tb, jb, jf, og = step - 5, step - 8, step - 9, step - 16
+            if step < NB - BPP:
+                gather(step // BPP + 1, step % BPP)
+            if 2 <= jb < NB + 2:
+                a_tok[jb] = work.tile([P, H, P], BF16, name="a_tok")
+            if 2 <= jf < NB + 2:
+                flip = psum.tile([P, H, P], BF16, name="bank")
+            for h in range(H):
+                if 1 <= tb <= NB:
+                    score(tb % NB, h)
+                if BPP <= step < NB and h < 2:
+                    name = ("q", "k")[h]
+                    acc = psum.tile([P, PIECE], F32, name="bank")
+                    for c in range(H):
+                        project_qk(name, step // BPP, step % BPP, c, acc)
+                    keep_qk(name, step // BPP, step % BPP, acc)
+                if step < NB and h == 2:
+                    project_v(step)
+                if 0 <= og < NB and h == 3:
+                    project_out(og // H, og % H)
+                if 2 <= jb < NB + 2:
+                    if h % 2 == 0:
+                        mix = psum.tile([P, 2, PIECE // 2], F32, name="bank")
+                    attend(jb % NB, h, mix)
+                    if h % 2 == 1:
+                        normalise(mix, a_tok[jb][:, h - 1 : h + 1, :])
+                if 2 <= jf < NB + 2:
+                    nc.tensor.transpose(flip[:, h, :], a_tok[jf][:, h, :], ident_bf[:])
+            if 1 <= tb <= NB:
+                mask(tb % NB)
+            if 2 <= jf < NB + 2:
+                nc.vector.tensor_copy(a_sb[:, :, (jf - 2) * P : (jf - 1) * P], flip[:])

@@ -40,13 +40,21 @@ def tile_slidingwindowattention_b_kernel(tc, x, wq, bq, wk, wv, bv, wo, bo, offs
         nc.sync.dma_start(offsets[:], offs)
         x_sb = [held.tile([P, N], F32, name=f"x{c}") for c in range(H)]
         w_sb = {name: held.tile([P, H, C], BF16, name=f"w{name}") for name in ("q", "k", "v", "o")}
-        nc.sync.dma_start(x_sb[0][:], x[0:P, :])
-        nc.sync.dma_start(w_sb["q"][:], wq.rearrange("(c p) m -> p c m", p=P))
-        nc.sync.dma_start(w_sb["k"][:], wk.rearrange("(c p) m -> p c m", p=P))
-        for c in range(1, H):
+
+        def load_x(c):
             nc.sync.dma_start(x_sb[c][:], x[c * P : (c + 1) * P, :])
-        nc.sync.dma_start(w_sb["v"][:], wv.rearrange("(c p) m -> p c m", p=P))
-        nc.sync.dma_start(w_sb["o"][:], wo.rearrange("(c p) m -> p c m", p=P))
+
+        def load_w(name, w):
+            nc.sync.dma_start(w_sb[name][:], w.rearrange("(c p) m -> p c m", p=P))
+
+        load_x(0)
+        load_w("q", wq)
+        load_x(1)
+        load_w("k", wk)
+        load_x(2)
+        load_x(3)
+        load_w("v", wv)
+        load_w("o", wo)
         b_sb = {}
         with nc.allow_non_contiguous_dma(reason="a bias lies one value to a partition"):
             for name, bias in (("v", bv), ("q", bq), ("o", bo)):
@@ -81,6 +89,19 @@ def tile_slidingwindowattention_b_kernel(tc, x, wq, bq, wk, wv, bv, wo, bo, offs
         a_sb = held.tile([P, H, N], BF16, name="a_sb")
         e_sb = [held.tile([P, H, SPAN], BF16, name=f"e{tb}") for tb in range(NB)]
         nc.vector.memset(v_sb[:, :, :, P : P + 1], 1.0)
+
+        band = held.tile([P, 2, P], BF16, name="band")
+        nc.gpsimd.memset(band[:], 1.0)
+        for side, sign in ((0, 1), (1, -1)):
+            nc.gpsimd.affine_select(
+                out=band[:, side, :],
+                in_=band[:, side, :],
+                pattern=[[sign, P]],
+                compare_op=ALU.is_ge,
+                fill=0.0,
+                base=0,
+                channel_multiplier=-sign,
+            )
 
         def gather(tp, c):
             xo32 = picked.tile([P, PIECE], F32)
@@ -139,24 +160,8 @@ def tile_slidingwindowattention_b_kernel(tc, x, wq, bq, wk, wv, bv, wo, bo, offs
             nc.scalar.activation(e_sb[tb][:, h, :], s_ps[:], ACT.Exp, scale=1.0 / math.sqrt(P))
 
         def mask(tb):
-            nc.gpsimd.affine_select(
-                out=e_sb[tb][:, :, 0:P],
-                in_=e_sb[tb][:, :, 0:P],
-                pattern=[[0, H], [1, P]],
-                compare_op=ALU.is_ge,
-                fill=0.0,
-                base=0,
-                channel_multiplier=-1,
-            )
-            nc.gpsimd.affine_select(
-                out=e_sb[tb][:, :, 2 * P : 3 * P],
-                in_=e_sb[tb][:, :, 2 * P : 3 * P],
-                pattern=[[0, H], [-1, P]],
-                compare_op=ALU.is_ge,
-                fill=0.0,
-                base=0,
-                channel_multiplier=1,
-            )
+            sides = e_sb[tb][:].rearrange("p h (s r) -> p h s r", s=3)[:, :, 0:3:2, :]
+            nc.vector.tensor_tensor(sides, sides, band[:].unsqueeze(1).to_broadcast([P, H, 2, P]), ALU.mult)
 
         def attend(jb, h, mix):
             for r in range(3):
@@ -208,8 +213,6 @@ def tile_slidingwindowattention_b_kernel(tc, x, wq, bq, wk, wv, bv, wo, bo, offs
                 gather(step // BPP + 1, step % BPP)
             if 2 <= jb < NB + 2:
                 a_tok[jb] = work.tile([P, H, P], BF16, name="a_tok")
-            if 2 <= jf < NB + 2:
-                flip = psum.tile([P, H, P], BF16, name="bank")
             for h in range(H):
                 if 1 <= tb <= NB:
                     score(tb % NB, h)
@@ -229,9 +232,10 @@ def tile_slidingwindowattention_b_kernel(tc, x, wq, bq, wk, wv, bv, wo, bo, offs
                     attend(jb % NB, h, mix)
                     if h % 2 == 1:
                         normalise(mix, a_tok[jb][:, h - 1 : h + 1, :])
-                if 2 <= jf < NB + 2:
-                    nc.tensor.transpose(flip[:, h, :], a_tok[jf][:, h, :], ident_bf[:])
             if 1 <= tb <= NB:
                 mask(tb % NB)
             if 2 <= jf < NB + 2:
+                flip = psum.tile([P, H, P], BF16, name="bank")
+                for h in range(H):
+                    nc.tensor.transpose(flip[:, h, :], a_tok[jf][:, h, :], ident_bf[:])
                 nc.vector.tensor_copy(a_sb[:, :, (jf - 2) * P : (jf - 1) * P], flip[:])

@@ -103,13 +103,16 @@ def tile_slidingwindowattention_b_kernel(tc, x, wq, bq, wk, wv, bv, wo, bo, offs
                 channel_multiplier=-sign,
             )
 
-        def gather(tp, c):
+        def look_up(tp, c):
             xo32 = picked.tile([P, PIECE], F32)
             nc.scalar.activation(
                 xo32[:],
                 x_sb[c][:].indirect(offsets[:, tp * (PIECE // 16) : (tp + 1) * (PIECE // 16)]),
                 ACT.Copy,
             )
+            return xo32
+
+        def round_xo(tp, c, xo32):
             nc.vector.tensor_copy(xo[:, c, tp * PIECE : (tp + 1) * PIECE], xo32[:])
 
         def project_qk(name, tp, m, c, acc):
@@ -200,17 +203,21 @@ def tile_slidingwindowattention_b_kernel(tc, x, wq, bq, wk, wv, bv, wo, bo, offs
 
         first_banks = [(name, m, psum.tile([P, PIECE], F32, name="bank")) for name in ("q", "k") for m in range(H)]
         for c in range(H):
-            gather(0, c)
+            round_xo(0, c, look_up(0, c))
             for name, m, acc in first_banks:
                 project_qk(name, 0, m, c, acc)
-        for name, m, acc in first_banks:
-            keep_qk(name, 0, m, acc)
+        for c in range(H):
+            xo32 = look_up(1, c)
+            for name, m, acc in first_banks[2 * c : 2 * c + 2]:
+                keep_qk(name, 0, m, acc)
+            round_xo(1, c, xo32)
 
         a_tok = {}
         for step in range(NB + 16):
             tb, jb, jf, og = step - 5, step - 8, step - 9, step - 16
-            if step < NB - BPP:
-                gather(step // BPP + 1, step % BPP)
+            looking = BPP <= step < NB - BPP
+            if looking:
+                xo32 = look_up(step // BPP + 1, step % BPP)
             if 2 <= jb < NB + 2:
                 a_tok[jb] = work.tile([P, H, P], BF16, name="a_tok")
             for h in range(H):
@@ -239,3 +246,5 @@ def tile_slidingwindowattention_b_kernel(tc, x, wq, bq, wk, wv, bv, wo, bo, offs
                 for h in range(H):
                     nc.tensor.transpose(flip[:, h, :], a_tok[jf][:, h, :], ident_bf[:])
                 nc.vector.tensor_copy(a_sb[:, :, (jf - 2) * P : (jf - 1) * P], flip[:])
+            if looking:
+                round_xo(step // BPP + 1, step % BPP, xo32)

@@ -47,12 +47,10 @@ def tile_slidingwindowattention_b_kernel(tc, x, wq, bq, wk, wv, bv, wo, bo, offs
         def load_w(name, w):
             nc.sync.dma_start(w_sb[name][:], w.rearrange("(c p) m -> p c m", p=P))
 
-        load_x(0)
-        load_w("q", wq)
-        load_x(1)
-        load_w("k", wk)
-        load_x(2)
-        load_x(3)
+        for c in range(H):
+            load_x(c)
+            for name, w in (("q", wq), ("k", wk)):
+                nc.sync.dma_start(w_sb[name][:, c, :], w[c * P : (c + 1) * P, :])
         load_w("v", wv)
         load_w("o", wo)
         b_sb = {}

@@ -180,24 +180,26 @@ def tile_slidingwindowattention_b_kernel(tc, x, wq, bq, wk, wv, bv, wo, bo, offs
             nc.vector.reciprocal(inv[:], mix[:, :, P : P + 1])
             nc.vector.tensor_tensor(a_pair, mix[:, :, 0:P], inv[:].to_broadcast([P, 2, P]), ALU.mult)
 
-        def project_out(g, m):
-            acc = psum.tile([P, PIECE], F32, name="bank")
-            for h in range(H):
-                nc.tensor.matmul(
-                    acc[:],
-                    lhsT=w_sb["o"][:, h, m * P : (m + 1) * P],
-                    rhs=a_sb[:, h, g * PIECE : (g + 1) * PIECE],
-                    start=(h == 0),
-                    stop=(h == H - 1),
-                )
+        def project_out(g, m, cuts=1):
             o_sb = staged.tile([P, PIECE], F32)
-            nc.scalar.activation(o_sb[:], acc[:], ACT.Identity, bias=b_sb["o"][:, m : m + 1])
-            at = 0
-            for first, count in ring_runs(g * BPP + 2, BPP):
-                nc.sync.dma_start(
-                    out[m * P : (m + 1) * P, first * P : (first + count) * P], o_sb[:, at : at + count * P]
-                )
-                at += count * P
+            for part in range(cuts):
+                lo, hi = part * PIECE // cuts, (part + 1) * PIECE // cuts
+                acc = psum.tile([P, hi - lo], F32, name="bank")
+                for h in range(H):
+                    nc.tensor.matmul(
+                        acc[:],
+                        lhsT=w_sb["o"][:, h, m * P : (m + 1) * P],
+                        rhs=a_sb[:, h, g * PIECE + lo : g * PIECE + hi],
+                        start=(h == 0),
+                        stop=(h == H - 1),
+                    )
+                nc.scalar.activation(o_sb[:, lo:hi], acc[:], ACT.Identity, bias=b_sb["o"][:, m : m + 1])
+                at = lo
+                for first, count in ring_runs(g * BPP + 2 + lo // P, (hi - lo) // P):
+                    nc.sync.dma_start(
+                        out[m * P : (m + 1) * P, first * P : (first + count) * P], o_sb[:, at : at + count * P]
+                    )
+                    at += count * P
 
         first_banks = [(name, m, psum.tile([P, PIECE], F32, name="bank")) for name in ("q", "k") for m in range(H)]
         for c in range(H):
@@ -230,7 +232,7 @@ def tile_slidingwindowattention_b_kernel(tc, x, wq, bq, wk, wv, bv, wo, bo, offs
                 if step < NB and h == 2:
                     project_v(step)
                 if 0 <= og < NB and h == 3:
-                    project_out(og // H, og % H)
+                    project_out(og // H, og % H, cuts=BPP if og == NB - 1 else 1)
                 if 2 <= jb < NB + 2:
                     if h % 2 == 0:
                         mix = psum.tile([P, 2, PIECE // 2], F32, name="bank")

@@ -101,25 +101,22 @@ def tile_slidingwindowattention_b_kernel(tc, x, wq, bq, wk, wv, bv, wo, bo, offs
                 channel_multiplier=-sign,
             )
 
-        def look_up(tp, c):
-            xo32 = picked.tile([P, PIECE], F32)
-            nc.scalar.activation(
-                xo32[:],
-                x_sb[c][:].indirect(offsets[:, tp * (PIECE // 16) : (tp + 1) * (PIECE // 16)]),
-                ACT.Copy,
-            )
+        def look_up(tp, c, part=slice(0, PIECE)):
+            lo, hi = tp * PIECE + part.start, tp * PIECE + part.stop
+            xo32 = picked.tile([P, hi - lo], F32)
+            nc.scalar.activation(xo32[:], x_sb[c][:].indirect(offsets[:, lo // 16 : hi // 16]), ACT.Copy)
             return xo32
 
-        def round_xo(tp, c, xo32):
-            nc.vector.tensor_copy(xo[:, c, tp * PIECE : (tp + 1) * PIECE], xo32[:])
+        def round_xo(tp, c, xo32, part=slice(0, PIECE)):
+            nc.vector.tensor_copy(xo[:, c, tp * PIECE + part.start : tp * PIECE + part.stop], xo32[:])
 
-        def project_qk(name, tp, m, c, acc):
+        def project_qk(name, tp, m, c, acc, part=slice(0, PIECE)):
             nc.tensor.matmul(
-                acc[:],
+                acc[:, part.start : part.stop],
                 lhsT=w_sb[name][:, c, m * P : (m + 1) * P],
-                rhs=xo[:, c, tp * PIECE : (tp + 1) * PIECE],
-                start=(c == 0),
-                stop=(c == H - 1),
+                rhs=xo[:, c, tp * PIECE + part.start : tp * PIECE + part.stop],
+                start=(c == 0 and part.start == 0),
+                stop=(c == H - 1 and part.stop == PIECE),
             )
 
         def keep_qk(name, tp, m, acc):
@@ -203,9 +200,10 @@ def tile_slidingwindowattention_b_kernel(tc, x, wq, bq, wk, wv, bv, wo, bo, offs
 
         first_banks = [(name, m, psum.tile([P, PIECE], F32, name="bank")) for name in ("q", "k") for m in range(H)]
         for c in range(H):
-            round_xo(0, c, look_up(0, c))
-            for name, m, acc in first_banks:
-                project_qk(name, 0, m, c, acc)
+            for part in (slice(0, PIECE // 2), slice(PIECE // 2, PIECE)):
+                round_xo(0, c, look_up(0, c, part), part)
+                for name, m, acc in first_banks:
+                    project_qk(name, 0, m, c, acc, part)
         for c in range(H):
             xo32 = look_up(1, c)
             for name, m, acc in first_banks[2 * c : 2 * c + 2]:

@@ -108,7 +108,11 @@ def tile_slidingwindowattention_b_kernel(tc, x, wq, bq, wk, wv, bv, wo, bo, offs
             return xo32
 
         def round_xo(tp, c, xo32, part=slice(0, PIECE)):
-            nc.vector.tensor_copy(xo[:, c, tp * PIECE + part.start : tp * PIECE + part.stop], xo32[:])
+            picked_bf = xo[:, c, tp * PIECE + part.start : tp * PIECE + part.stop]
+            if tp == 0:
+                nc.vector.tensor_copy(picked_bf, xo32[:])
+            else:
+                nc.gpsimd.tensor_scalar_mul(picked_bf, xo32[:], 1.0)
 
         def project_qk(name, tp, m, c, acc, part=slice(0, PIECE)):
             nc.tensor.matmul(
@@ -198,17 +202,22 @@ def tile_slidingwindowattention_b_kernel(tc, x, wq, bq, wk, wv, bv, wo, bo, offs
                     )
                     at += count * P
 
-        first_banks = [(name, m, psum.tile([P, PIECE], F32, name="bank")) for name in ("q", "k") for m in range(H)]
+        heads = [(name, m) for name in ("q", "k") for m in range(H)]
+        first_banks = [(name, m, psum.tile([P, PIECE], F32, name="bank")) for name, m in heads[:-1]]
         for c in range(H):
             for part in (slice(0, PIECE // 2), slice(PIECE // 2, PIECE)):
                 round_xo(0, c, look_up(0, c, part), part)
                 for name, m, acc in first_banks:
                     project_qk(name, 0, m, c, acc, part)
+        name, m = heads[-1]
+        acc = psum.tile([P, PIECE], F32, name="bank")
         for c in range(H):
-            xo32 = look_up(1, c)
-            for name, m, acc in first_banks[2 * c : 2 * c + 2]:
-                keep_qk(name, 0, m, acc)
-            round_xo(1, c, xo32)
+            project_qk(name, 0, m, c, acc)
+        first_banks.append((name, m, acc))
+        for c in range(H):
+            round_xo(1, c, look_up(1, c))
+        for name, m, acc in first_banks:
+            keep_qk(name, 0, m, acc)
 
         a_tok = {}
         for step in range(NB + 16):

@@ -112,7 +112,7 @@ def tile_slidingwindowattention_b_kernel(tc, x, wq, bq, wk, wv, bv, wo, bo, offs
             if tp == 0:
                 nc.vector.tensor_copy(picked_bf, xo32[:])
             else:
-                nc.gpsimd.tensor_scalar_mul(picked_bf, xo32[:], 1.0)
+                nc.gpsimd.tensor_copy(picked_bf, xo32[:])
 
         def project_qk(name, tp, m, c, acc, part=slice(0, PIECE)):
             nc.tensor.matmul(

@@ -51,13 +51,18 @@ def tile_slidingwindowattention_b_kernel(tc, x, wq, bq, wk, wv, bv, wo, bo, offs
             load_x(c)
             for name, w in (("q", wq), ("k", wk)):
                 nc.sync.dma_start(w_sb[name][:, c, :], w[c * P : (c + 1) * P, :])
+        b_sb = {}
+
+        def load_bias(queue, name, bias):
+            b_sb[name] = held.tile([P, H], F32, name=f"b{name}")
+            with nc.allow_non_contiguous_dma(reason="a bias lies one value to a partition"):
+                queue.dma_start(b_sb[name][:], bias.rearrange("(a p) o -> p (a o)", p=P))
+
+        load_bias(nc.scalar, "v", bv)
+        load_bias(nc.sync, "q", bq)
         load_w("v", wv)
         load_w("o", wo)
-        b_sb = {}
-        with nc.allow_non_contiguous_dma(reason="a bias lies one value to a partition"):
-            for name, bias in (("v", bv), ("q", bq), ("o", bo)):
-                b_sb[name] = held.tile([P, H], F32, name=f"b{name}")
-                nc.scalar.dma_start(b_sb[name][:], bias.rearrange("(a p) o -> p (a o)", p=P))
+        load_bias(nc.sync, "o", bo)
 
         warm = held.tile([P, 1], F32, name="warm")
         nc.vector.memset(warm[:], 0.0)

import math

import concourse.mybir as mybir
from concourse.masks import make_identity

F32, BF16, U16 = mybir.dt.float32, mybir.dt.bfloat16, mybir.dt.uint16
ACT = mybir.ActivationFunctionType
ALU = mybir.AluOpType

P = 128
C = 512
N = 2048
H = C // P
NB = N // P
PIECE = 512
BPP = PIECE // P
SPAN = 3 * P
VW = 136

FLOPS = 4 * 2 * C * C * N + 2 * 2 * H * N * 257 * P


def ring_runs(first, count):
    first = first % NB
    if first + count <= NB:
        return [(first, count)]
    return [(first, NB - first), (0, first + count - NB)]


def tile_slidingwindowattention_b_kernel(tc, x, wq, bq, wk, wv, bv, wo, bo, offs, out):
    nc = tc.nc
    with (
        tc.tile_pool(name="held", bufs=1) as held,
        tc.tile_pool(name="picked", bufs=4) as picked,
        tc.tile_pool(name="work", bufs=3) as work,
        tc.tile_pool(name="staged", bufs=4) as staged,
        tc.psum_pool(name="psum", bufs=8) as psum,
    ):
        offsets = held.tile([P, N // 16], U16, name="offsets")
        nc.sync.dma_start(offsets[:], offs)
        x_sb = [held.tile([P, N], F32, name=f"x{c}") for c in range(H)]
        w_sb = {name: held.tile([P, H, C], BF16, name=f"w{name}") for name in ("q", "k", "v", "o")}

        def load_x(c):
            nc.sync.dma_start(x_sb[c][:], x[c * P : (c + 1) * P, :])

        def load_w(name, w):
            nc.sync.dma_start(w_sb[name][:], w.rearrange("(c p) m -> p c m", p=P))

        for c in range(H):
            load_x(c)
            for name, w in (("q", wq), ("k", wk)):
                nc.sync.dma_start(w_sb[name][:, c, :], w[c * P : (c + 1) * P, :])
        b_sb = {}

        def load_bias(queue, name, bias):
            b_sb[name] = held.tile([P, H], F32, name=f"b{name}")
            with nc.allow_non_contiguous_dma(reason="a bias lies one value to a partition"):
                queue.dma_start(b_sb[name][:], bias.rearrange("(a p) o -> p (a o)", p=P))

        load_bias(nc.scalar, "v", bv)
        load_bias(nc.sync, "q", bq)
        load_w("v", wv)
        load_w("o", wo)
        load_bias(nc.sync, "o", bo)

        warm = held.tile([P, 1], F32, name="warm")
        nc.vector.memset(warm[:], 0.0)
        nc.scalar.activation(warm[:], warm[:], ACT.Exp)

        ident_f32 = held.tile([P, P], F32, name="ident_f32")
        make_identity(nc, ident_f32[:])
        ident_bf = held.tile([P, P], BF16, name="ident_bf")
        make_identity(nc, ident_bf[:])

        acc = psum.tile([P, PIECE], F32, name="bank")
        for h in range(H):
            nc.tensor.matmul(
                acc[:, h * P : (h + 1) * P],
                lhsT=b_sb["v"][:, h : h + 1].to_broadcast([P, P]),
                rhs=ident_f32[:],
                start=True,
                stop=True,
            )
        bv_all = held.tile([P, C], F32, name="bv_all")
        nc.vector.tensor_copy(bv_all[:], acc[:])

        xo = held.tile([P, H, N], BF16, name="xo")
        q_sb = held.tile([P, H, N], BF16, name="q_sb")
        k_sb = held.tile([P, H, N], BF16, name="k_sb")
        v_sb = held.tile([P, NB, H, VW], BF16, name="v_sb")
        a_sb = held.tile([P, H, N], BF16, name="a_sb")
        e_sb = [held.tile([P, H, SPAN], BF16, name=f"e{tb}") for tb in range(NB)]
        nc.vector.memset(v_sb[:, :, :, P : P + 1], 1.0)

        band = held.tile([P, 2, P], BF16, name="band")
        nc.gpsimd.memset(band[:], 1.0)
        for side, sign in ((0, 1), (1, -1)):
            nc.gpsimd.affine_select(
                out=band[:, side, :],
                in_=band[:, side, :],
                pattern=[[sign, P]],
                compare_op=ALU.is_ge,
                fill=0.0,
                base=0,
                channel_multiplier=-sign,
            )

        def look_up(tp, c, part=slice(0, PIECE)):
            lo, hi = tp * PIECE + part.start, tp * PIECE + part.stop
            xo32 = picked.tile([P, hi - lo], F32)
            nc.scalar.activation(xo32[:], x_sb[c][:].indirect(offsets[:, lo // 16 : hi // 16]), ACT.Copy)
            return xo32

        def round_xo(tp, c, xo32, part=slice(0, PIECE)):
            picked_bf = xo[:, c, tp * PIECE + part.start : tp * PIECE + part.stop]
            if tp == 0:
                nc.vector.tensor_copy(picked_bf, xo32[:])
            else:
                nc.gpsimd.tensor_copy(picked_bf, xo32[:])

        def project_qk(name, tp, m, c, acc, part=slice(0, PIECE)):
            nc.tensor.matmul(
                acc[:, part.start : part.stop],
                lhsT=w_sb[name][:, c, m * P : (m + 1) * P],
                rhs=xo[:, c, tp * PIECE + part.start : tp * PIECE + part.stop],
                start=(c == 0 and part.start == 0),
                stop=(c == H - 1 and part.stop == PIECE),
            )

        def keep_qk(name, tp, m, acc):
            cols = slice(tp * PIECE, (tp + 1) * PIECE)
            if name == "q":
                nc.vector.tensor_scalar_add(q_sb[:, m, cols], acc[:], b_sb["q"][:, m : m + 1])
            else:
                nc.vector.tensor_copy(k_sb[:, m, cols], acc[:])

        def project_v(tb):
            acc = psum.tile([P, PIECE], F32, name="bank")
            for c in range(H):
                nc.tensor.matmul(
                    acc[:],
                    lhsT=xo[:, c, tb * P : (tb + 1) * P],
                    rhs=w_sb["v"][:, c, :],
                    start=(c == 0),
                    stop=(c == H - 1),
                )
            nc.vector.tensor_tensor(
                v_sb[:, tb, :, 0:P],
                acc[:].rearrange("p (h d) -> p h d", h=H),
                bv_all[:].rearrange("p (h d) -> p h d", h=H),
                ALU.add,
            )

        def score(tb, h):
            s_ps = psum.tile([P, SPAN], F32, name="bank")
            at = 0
            for first, count in ring_runs(tb - 1, 3):
                nc.tensor.matmul(
                    s_ps[:, at : at + count * P],
                    lhsT=k_sb[:, h, tb * P : (tb + 1) * P],
                    rhs=q_sb[:, h, first * P : (first + count) * P],
                    start=True,
                    stop=True,
                )
                at += count * P
            nc.scalar.activation(e_sb[tb][:, h, :], s_ps[:], ACT.Exp, scale=1.0 / math.sqrt(P))

        def mask(tb):
            sides = e_sb[tb][:].rearrange("p h (s r) -> p h s r", s=3)[:, :, 0:3:2, :]
            nc.vector.tensor_tensor(sides, sides, band[:].unsqueeze(1).to_broadcast([P, H, 2, P]), ALU.mult)

        def attend(jb, h, mix):
            for r in range(3):
                tb = (jb - 1 + r) % NB
                nc.tensor.matmul(
                    mix[:, h % 2, 0 : P + 1],
                    lhsT=e_sb[tb][:, h, (2 - r) * P : (3 - r) * P],
                    rhs=v_sb[:, tb, h, 0 : P + 1],
                    start=(r == 0),
                    stop=(r == 2),
                )

        def normalise(mix, a_pair):
            inv = work.tile([P, 2, 1], F32)
            nc.vector.reciprocal(inv[:], mix[:, :, P : P + 1])
            nc.vector.tensor_tensor(a_pair, mix[:, :, 0:P], inv[:].to_broadcast([P, 2, P]), ALU.mult)

        def project_out(g, m, cuts=1):
            o_sb = staged.tile([P, PIECE], F32)
            for part in range(cuts):
                lo, hi = part * PIECE // cuts, (part + 1) * PIECE // cuts
                acc = psum.tile([P, hi - lo], F32, name="bank")
                for h in range(H):
                    nc.tensor.matmul(
                        acc[:],
                        lhsT=w_sb["o"][:, h, m * P : (m + 1) * P],
                        rhs=a_sb[:, h, g * PIECE + lo : g * PIECE + hi],
                        start=(h == 0),
                        stop=(h == H - 1),
                    )
                nc.scalar.activation(o_sb[:, lo:hi], acc[:], ACT.Identity, bias=b_sb["o"][:, m : m + 1])
                at = lo
                for first, count in ring_runs(g * BPP + 2 + lo // P, (hi - lo) // P):
                    nc.sync.dma_start(
                        out[m * P : (m + 1) * P, first * P : (first + count) * P], o_sb[:, at : at + count * P]
                    )
                    at += count * P

        heads = [(name, m) for name in ("q", "k") for m in range(H)]
        first_banks = [(name, m, psum.tile([P, PIECE], F32, name="bank")) for name, m in heads[:-1]]
        for c in range(H):
            for part in (slice(0, PIECE // 2), slice(PIECE // 2, PIECE)):
                round_xo(0, c, look_up(0, c, part), part)
                for name, m, acc in first_banks:
                    project_qk(name, 0, m, c, acc, part)
        name, m = heads[-1]
        acc = psum.tile([P, PIECE], F32, name="bank")
        for c in range(H):
            project_qk(name, 0, m, c, acc)
        first_banks.append((name, m, acc))
        for c in range(H):
            round_xo(1, c, look_up(1, c))
        for name, m, acc in first_banks:
            keep_qk(name, 0, m, acc)

        a_tok = {}
        for step in range(NB + 16):
            tb, jb, jf, og = step - 5, step - 8, step - 9, step - 16
            looking = BPP <= step < NB - BPP
            if looking:
                xo32 = look_up(step // BPP + 1, step % BPP)
            if 2 <= jb < NB + 2:
                a_tok[jb] = work.tile([P, H, P], BF16, name="a_tok")
            for h in range(H):
                if 1 <= tb <= NB:
                    score(tb % NB, h)
                if BPP <= step < NB and h < 2:
                    name = ("q", "k")[h]
                    acc = psum.tile([P, PIECE], F32, name="bank")
                    for c in range(H):
                        project_qk(name, step // BPP, step % BPP, c, acc)
                    keep_qk(name, step // BPP, step % BPP, acc)
                if step < NB and h == 2:
                    project_v(step)
                if 0 <= og < NB and h == 3:
                    project_out(og // H, og % H, cuts=BPP if og == NB - 1 else 1)
                if 2 <= jb < NB + 2:
                    if h % 2 == 0:
                        mix = psum.tile([P, 2, PIECE // 2], F32, name="bank")
                    attend(jb % NB, h, mix)
                    if h % 2 == 1:
                        normalise(mix, a_tok[jb][:, h - 1 : h + 1, :])
            if 1 <= tb <= NB:
                mask(tb % NB)
            if 2 <= jf < NB + 2:
                flip = psum.tile([P, H, P], BF16, name="bank")
                for h in range(H):
                    nc.tensor.transpose(flip[:, h, :], a_tok[jf][:, h, :], ident_bf[:])
                nc.vector.tensor_copy(a_sb[:, :, (jf - 2) * P : (jf - 1) * P], flip[:])
            if looking:
                round_xo(step // BPP + 1, step % BPP, xo32)
